import numpy as np
import ml_dtypes


def mxq(x, axis, fmt="e4m3"):
    dtype, down = {"e4m3": (ml_dtypes.float8_e4m3fn, 7), "e5m2": (ml_dtypes.float8_e5m2, 14)}[fmt]
    v = np.moveaxis(np.asarray(x, np.float32).astype(ml_dtypes.bfloat16).astype(np.float64), axis, -1)
    blocks = v.reshape(v.shape[:-1] + (-1, 32))
    amax = np.abs(blocks).max(-1, keepdims=True)
    byte = np.maximum(np.where(amax > 0, np.frexp(amax)[1] - 1 + 127, 0) - down, 1)
    scale = np.exp2(byte - 127.0)
    codes = (blocks / scale).astype(np.float32).astype(dtype).astype(np.float64)
    return np.moveaxis((codes * scale).reshape(v.shape), -1, axis)


WIDE = False


def mx_kscale(k):
    if not WIDE:
        return np.ones(k)
    levels = np.array([10, -10, 5, -5, 0])
    a = np.random.permutation(np.resize(levels, k // 512 * 4)).reshape(k // 512, 4)
    idx = np.arange(k)
    return np.exp2(a[idx // 512, idx % 128 // 32])


BF16 = ml_dtypes.bfloat16


def bf(x):
    return np.asarray(x, np.float32).astype(BF16)


def f64(x):
    return np.asarray(x).astype(np.float64)


B, S, H, I, G = 4, 1024, 512, 1024, 4
T = B * S


def grouped_linear(xf, w, b):
    g, dout, din = w.shape
    xg = xf.reshape(g, -1, din)
    y = (mxq(xg, 2, "e4m3") @ mxq(w, 2, "e4m3").transpose(0, 2, 1)) + b[:, None, :]
    return y.reshape(-1, dout)


def setup_inputs():
    s, t = mx_kscale(H), mx_kscale(I)
    return {"hf": bf(np.random.standard_normal((T, H)) * s),
            "g1_w": bf(np.random.standard_normal((G, I, H)) / np.sqrt(H) / s[None, None, :] * t[None, :, None]),
            "g1_b": bf(np.random.standard_normal((G, I)) * 0.3 * t[None, :]),
            "g2_w": bf(np.random.standard_normal((G, H, I)) / np.sqrt(I) / t[None, None, :]),
            "g2_b": bf(np.random.standard_normal((G, H)) * 0.3)}


def reference(hf, g1_w, g1_b, g2_w, g2_b):
    y = grouped_linear(f64(hf), f64(g1_w), f64(g1_b))
    return grouped_linear(y, f64(g2_w), f64(g2_b))

@@ -1,0 +1,230 @@
+from contextlib import ExitStack
+
+import concourse.mybir as mybir
+from concourse.masks import make_identity
+
+F32 = mybir.dt.float32
+BF16 = mybir.dt.bfloat16
+U32 = mybir.dt.uint32
+U8 = mybir.dt.uint8
+FP8X4 = mybir.dt.float8_e4m3fn_x4
+
+P = 128
+PACK = 4
+K_PASS = P * PACK
+WORDS = K_PASS // 2
+
+GROUPS, TOKENS, HIDDEN, INNER = 4, 4096, 512, 1024
+GROUP_TOKENS = TOKENS // GROUPS
+CHUNK = 512
+CHUNKS = TOKENS // CHUNK
+CHUNKS_PER_GROUP = GROUP_TOKENS // CHUNK
+BLOCKS = CHUNK // P
+TOKEN_STEP = GROUP_TOKENS // P
+PASSES_2 = INNER // K_PASS
+INNER_TILES = INNER // P
+
+LEAD = 4
+UNITS_PER_ROUND = 3
+
+FLOPS = 2 * TOKENS * HIDDEN * INNER * 2
+
+
+def tile_dummytemodel_pa_t_kernel(tc, hf, g1_w, g1_b, g2_w, g2_b, out):
+    nc = tc.nc
+    with ExitStack() as ctx:
+        const = ctx.enter_context(tc.tile_pool(name="const", bufs=1))
+        inputs = ctx.enter_context(tc.tile_pool(name="inputs", bufs=1))
+        grouped_pool = ctx.enter_context(tc.tile_pool(name="grouped", bufs=3))
+        codes_pool = ctx.enter_context(tc.tile_pool(name="codes", bufs=4))
+        y_pool = ctx.enter_context(tc.tile_pool(name="y", bufs=3))
+        out_pool = ctx.enter_context(tc.tile_pool(name="outs", bufs=6))
+        psum_t = ctx.enter_context(tc.psum_pool(name="psum_t", bufs=2))
+        psum_1 = ctx.enter_context(tc.psum_pool(name="psum_1", bufs=4))
+        psum_2 = ctx.enter_context(tc.psum_pool(name="psum_2", bufs=2))
+
+        hf_view = hf.rearrange("(g r a) k -> g r a k", g=GROUPS, r=P)
+        out_view = out.rearrange("(g r a) h -> g r a h", g=GROUPS, r=P)
+        w1_view = g1_w.rearrange("g (cu r e) k -> g r cu (e k)", r=P, e=2)
+        w2_view = g2_w.rearrange("g (b r) i -> g r b i", r=P)
+
+        x_sb = [inputs.tile([P, BLOCKS, HIDDEN], BF16, name="x_sb%d" % s) for s in range(CHUNKS)]
+        w1_sb = [inputs.tile([P, INNER_TILES, HIDDEN], BF16, name="w1_sb%d" % g) for g in range(GROUPS)]
+        w2_sb = [inputs.tile([P, HIDDEN // P, INNER], BF16, name="w2_sb%d" % g) for g in range(GROUPS)]
+
+        b1_rows = const.tile([P, P], F32)
+        nc.vector.memset(b1_rows[:], 0.0)
+        nc.scalar.dma_start(
+            out=b1_rows[:].bitcast(BF16)[0 : GROUPS * 4, :],
+            in_=g1_b.rearrange("g (cu w) -> (g cu) w", w=2 * P),
+        )
+        b2_all = const.tile([P, GROUPS * HIDDEN], BF16)
+
+        def load_x(s):
+            g, n = divmod(s, CHUNKS_PER_GROUP)
+            nc.sync.dma_start(out=x_sb[s][:], in_=hf_view[g, :, n * BLOCKS : (n + 1) * BLOCKS, :])
+
+        for g in range(GROUPS):
+            load_x(CHUNKS_PER_GROUP * g)
+            for c in range(PASSES_2):
+                nc.sync.dma_start(
+                    out=w1_sb[g][:, 4 * c : 4 * c + 4, :].rearrange("p (cu e) k -> p cu (e k)", e=2),
+                    in_=w1_view[g, :, 2 * c : 2 * c + 2, :],
+                )
+            load_x(CHUNKS_PER_GROUP * g + 1)
+            nc.sync.dma_start(out=w2_sb[g][:], in_=w2_view[g])
+            if g == 0:
+                nc.sync.dma_start(out=b2_all[:], in_=g2_b.rearrange("g h -> (g h)").partition_broadcast(P))
+
+        ident = const.tile([P, P], F32)
+        make_identity(nc, ident[:])
+
+        b1_bank = psum_t.tile([P, 2, 2, P], F32, tag="bank")
+        nc.tensor.transpose(b1_bank[:, 0, 0, :], b1_rows[:], ident[:])
+        b1_words = const.tile([P, GROUPS * 4], F32)
+        nc.vector.tensor_copy(out=b1_words[:], in_=b1_bank[:, 0, 0, 0 : GROUPS * 4])
+        b1_col = const.tile([P, GROUPS * INNER_TILES], F32)
+        nc.vector.tensor_copy(out=b1_col[:], in_=b1_words[:].bitcast(BF16))
+
+        def unit_blocks(key):
+            kind = key[0]
+            if kind == "x":
+                words = x_sb[key[1]][:].bitcast(F32)
+                return [words[:, a, :] for a in range(BLOCKS)]
+            if kind == "w1":
+                words = w1_sb[key[1]][:].bitcast(F32)
+                return [words[:, PACK * key[2] + j, :] for j in range(PACK)]
+            words = w2_sb[key[1]][:].bitcast(F32)
+            return [words[:, b, WORDS * key[2] : WORDS * (key[2] + 1)] for b in range(HIDDEN // P)]
+
+        grouped = {}
+        codes = {}
+
+        def transpose_unit(key):
+            blocks = unit_blocks(key)
+            unit_bf16 = grouped_pool.tile([P, CHUNK, PACK], BF16, tag="unit_bf16", align_bytes=64)
+            unit_words = unit_bf16[:].bitcast(F32)
+            for half in range(2):
+                bank = psum_t.tile([P, 2, 2, P], F32, tag="bank")
+                for b in range(2):
+                    for u in range(2):
+                        nc.tensor.transpose(bank[:, b, u, :], blocks[2 * half + b][:, u * P : (u + 1) * P], ident[:])
+                nc.scalar.copy(
+                    out=unit_words[:, 2 * P * half : 2 * P * (half + 1), :].rearrange("p (b r) u -> p b r u", b=2),
+                    in_=bank[:].rearrange("p b u r -> p b r u"),
+                )
+            grouped[key] = unit_bf16
+
+        def quantise(key, tag):
+            words = codes_pool.tile([P, CHUNK], U32, tag=tag + "_words", align_bytes=64)
+            scales = codes_pool.tile([P, CHUNK], U8, tag=tag + "_scales", align_bytes=64)
+            nc.vector.quantize_mx(
+                out=words[:].bitcast(FP8X4),
+                scales=scales[:],
+                in_=grouped[key][:].rearrange("p c j -> p (c j)"),
+            )
+            codes[key] = (words, scales)
+
+        planar = {}
+
+        def layer1(s, c):
+            g = s // CHUNKS_PER_GROUP
+            x_words, x_scales = codes[("x", s)]
+            w_words, w_scales = codes[("w1", g, c)]
+            y_planar = y_pool.tile([P, PACK, CHUNK], BF16, tag="y_planar")
+            for j in range(PACK):
+                acc1 = psum_1.tile([P, CHUNK], F32, tag="acc1")
+                nc.tensor.matmul_mx(
+                    out=acc1[:],
+                    lhsT=w_words[:, j * P : (j + 1) * P].bitcast(FP8X4),
+                    lhsT_scale=w_scales[:, j * P : (j + 1) * P],
+                    rhs=x_words[:].bitcast(FP8X4),
+                    rhs_scale=x_scales[:],
+                    start=True,
+                    stop=True,
+                )
+                column = INNER_TILES * g + PACK * c + j
+                nc.scalar.activation(
+                    out=y_planar[:, j, :],
+                    in_=acc1[:],
+                    func=mybir.ActivationFunctionType.Identity,
+                    bias=b1_col[:, column : column + 1],
+                )
+            planar[(s, c)] = y_planar
+
+        def regroup_y(s, c):
+            y_bf16 = y_pool.tile([P, CHUNK, PACK], BF16, tag="y_bf16", align_bytes=64)
+            nc.vector.tensor_copy(
+                out=y_bf16[:].rearrange("p (t i) j -> p t j i", i=4),
+                in_=planar[(s, c)][:].rearrange("p j (t i) -> p t j i", i=4),
+            )
+            grouped[("y", s, c)] = y_bf16
+
+        def layer2(s, blocks):
+            g, n = divmod(s, CHUNKS_PER_GROUP)
+            for b in blocks:
+                acc2 = psum_2.tile([P, HIDDEN], F32, tag="acc2")
+                for c in range(PASSES_2):
+                    y_words, y_scales = codes[("y", s, c)]
+                    w_words, w_scales = codes[("w2", g, c)]
+                    nc.tensor.matmul_mx(
+                        out=acc2[:],
+                        lhsT=y_words[:, b * P : (b + 1) * P].bitcast(FP8X4),
+                        lhsT_scale=y_scales[:, b * P : (b + 1) * P],
+                        rhs=w_words[:].bitcast(FP8X4),
+                        rhs_scale=w_scales[:],
+                        start=(c == 0),
+                        stop=(c == PASSES_2 - 1),
+                    )
+                result = out_pool.tile([P, HIDDEN], F32, tag="result")
+                nc.vector.tensor_tensor(
+                    out=result[:],
+                    in0=acc2[:],
+                    in1=b2_all[:, g * HIDDEN : (g + 1) * HIDDEN],
+                    op=mybir.AluOpType.add,
+                )
+                nc.sync.dma_start(out=out_view[g, :, n * BLOCKS + b, :], in_=result[:])
+
+        units = []
+        for g in range(GROUPS):
+            units.append(("x", CHUNKS_PER_GROUP * g))
+            units.extend([("w1", g, c) for c in range(PASSES_2)])
+            units.append(("x", CHUNKS_PER_GROUP * g + 1))
+            units.extend([("w2", g, c) for c in range(PASSES_2)])
+
+        for i in range(LEAD):
+            transpose_unit(units[i])
+            if i > 0:
+                quantise(units[i - 1], units[i - 1][0])
+        quantise(units[LEAD - 1], units[LEAD - 1][0])
+
+        for s in range(CHUNKS + 1):
+            first = LEAD + UNITS_PER_ROUND * s
+            unit_a, unit_b, unit_c = units[first : first + 1], units[first + 1 : first + 2], units[first + 2 : first + 3]
+            if s < CHUNKS:
+                layer1(s, 0)
+            for key in unit_a:
+                transpose_unit(key)
+            if s < CHUNKS:
+                regroup_y(s, 0)
+                layer1(s, 1)
+            for key in unit_a:
+                quantise(key, key[0])
+            for key in unit_b:
+                transpose_unit(key)
+            if s < CHUNKS:
+                quantise(("y", s, 0), "y")
+            if s > 0:
+                layer2(s - 1, range(0, BLOCKS // 2))
+            if s < CHUNKS:
+                regroup_y(s, 1)
+            for key in unit_b:
+                quantise(key, key[0])
+            if s > 0:
+                layer2(s - 1, range(BLOCKS // 2, BLOCKS))
+            for key in unit_c:
+                transpose_unit(key)
+            if s < CHUNKS:
+                quantise(("y", s, 1), "y")
+            for key in unit_c:
+                quantise(key, key[0])

@@ -13,6 +13,7 @@ P = 128
 PACK = 4
 K_PASS = P * PACK
 WORDS = K_PASS // 2
+BANK = 512
 
 GROUPS, TOKENS, HIDDEN, INNER = 4, 4096, 512, 1024
 GROUP_TOKENS = TOKENS // GROUPS
@@ -20,12 +21,12 @@ CHUNK = 512
 CHUNKS = TOKENS // CHUNK
 CHUNKS_PER_GROUP = GROUP_TOKENS // CHUNK
 BLOCKS = CHUNK // P
-TOKEN_STEP = GROUP_TOKENS // P
 PASSES_2 = INNER // K_PASS
 INNER_TILES = INNER // P
 
 LEAD = 4
 UNITS_PER_ROUND = 3
+ROUNDS_WITH_HELP = 1
 
 FLOPS = 2 * TOKENS * HIDDEN * INNER * 2
 
@@ -39,9 +40,9 @@ def tile_dummytemodel_pa_t_kernel(tc, hf, g1_w, g1_b, g2_w, g2_b, out):
         codes_pool = ctx.enter_context(tc.tile_pool(name="codes", bufs=4))
         y_pool = ctx.enter_context(tc.tile_pool(name="y", bufs=3))
         out_pool = ctx.enter_context(tc.tile_pool(name="outs", bufs=6))
-        psum_t = ctx.enter_context(tc.psum_pool(name="psum_t", bufs=2))
-        psum_1 = ctx.enter_context(tc.psum_pool(name="psum_1", bufs=4))
-        psum_2 = ctx.enter_context(tc.psum_pool(name="psum_2", bufs=2))
+        psum_scalar = ctx.enter_context(tc.psum_pool(name="psum_scalar", bufs=5))
+        psum_vector = ctx.enter_context(tc.psum_pool(name="psum_vector", bufs=3))
+        ctx.enter_context(tc.manual_schedule())
 
         hf_view = hf.rearrange("(g r a) k -> g r a k", g=GROUPS, r=P)
         out_view = out.rearrange("(g r a) h -> g r a h", g=GROUPS, r=P)
@@ -62,15 +63,23 @@ def tile_dummytemodel_pa_t_kernel(tc, hf, g1_w, g1_b, g2_w, g2_b, out):
 
         def load_x(s):
             g, n = divmod(s, CHUNKS_PER_GROUP)
-            nc.sync.dma_start(out=x_sb[s][:], in_=hf_view[g, :, n * BLOCKS : (n + 1) * BLOCKS, :])
+            for half in range(2):
+                nc.sync.dma_start(
+                    out=x_sb[s][:, 2 * half : 2 * half + 2, :],
+                    in_=hf_view[g, :, n * BLOCKS + 2 * half : n * BLOCKS + 2 * half + 2, :],
+                )
+
+        def load_w1(g, c):
+            for u in range(2):
+                nc.sync.dma_start(
+                    out=w1_sb[g][:, PACK * c + 2 * u : PACK * c + 2 * u + 2, :].rearrange("p e k -> p (e k)"),
+                    in_=w1_view[g, :, 2 * c + u, :],
+                )
 
         for g in range(GROUPS):
             load_x(CHUNKS_PER_GROUP * g)
             for c in range(PASSES_2):
-                nc.sync.dma_start(
-                    out=w1_sb[g][:, 4 * c : 4 * c + 4, :].rearrange("p (cu e) k -> p cu (e k)", e=2),
-                    in_=w1_view[g, :, 2 * c : 2 * c + 2, :],
-                )
+                load_w1(g, c)
             load_x(CHUNKS_PER_GROUP * g + 1)
             nc.sync.dma_start(out=w2_sb[g][:], in_=w2_view[g])
             if g == 0:
@@ -79,12 +88,14 @@ def tile_dummytemodel_pa_t_kernel(tc, hf, g1_w, g1_b, g2_w, g2_b, out):
         ident = const.tile([P, P], F32)
         make_identity(nc, ident[:])
 
-        b1_bank = psum_t.tile([P, 2, 2, P], F32, tag="bank")
-        nc.tensor.transpose(b1_bank[:, 0, 0, :], b1_rows[:], ident[:])
         b1_words = const.tile([P, GROUPS * 4], F32)
-        nc.vector.tensor_copy(out=b1_words[:], in_=b1_bank[:, 0, 0, 0 : GROUPS * 4])
         b1_col = const.tile([P, GROUPS * INNER_TILES], F32)
-        nc.vector.tensor_copy(out=b1_col[:], in_=b1_words[:].bitcast(BF16))
+
+        def transpose_bias():
+            b1_bank = psum_scalar.tile([P, BANK], F32, tag="bank")
+            nc.tensor.transpose(b1_bank[:, 0:P], b1_rows[:], ident[:])
+            nc.vector.tensor_copy(out=b1_words[:], in_=b1_bank[:, 0 : GROUPS * 4])
+            nc.vector.tensor_copy(out=b1_col[:], in_=b1_words[:].bitcast(BF16))
 
         def unit_blocks(key):
             kind = key[0]
@@ -105,17 +116,19 @@ def tile_dummytemodel_pa_t_kernel(tc, hf, g1_w, g1_b, g2_w, g2_b, out):
             unit_bf16 = grouped_pool.tile([P, CHUNK, PACK], BF16, tag="unit_bf16", align_bytes=64)
             unit_words = unit_bf16[:].bitcast(F32)
             for half in range(2):
-                bank = psum_t.tile([P, 2, 2, P], F32, tag="bank")
+                bank = psum_scalar.tile([P, BANK], F32, tag="bank")
+                planes = bank[:].rearrange("p (b u r) -> p b u r", b=2, u=2)
                 for b in range(2):
                     for u in range(2):
-                        nc.tensor.transpose(bank[:, b, u, :], blocks[2 * half + b][:, u * P : (u + 1) * P], ident[:])
+                        nc.tensor.transpose(planes[:, b, u, :], blocks[2 * half + b][:, u * P : (u + 1) * P], ident[:])
                 nc.scalar.copy(
                     out=unit_words[:, 2 * P * half : 2 * P * (half + 1), :].rearrange("p (b r) u -> p b r u", b=2),
-                    in_=bank[:].rearrange("p b u r -> p b r u"),
+                    in_=planes.rearrange("p b u r -> p b r u"),
                 )
             grouped[key] = unit_bf16
 
-        def quantise(key, tag):
+        def quantise(key):
+            tag = key[0]
             words = codes_pool.tile([P, CHUNK], U32, tag=tag + "_words", align_bytes=64)
             scales = codes_pool.tile([P, CHUNK], U8, tag=tag + "_scales", align_bytes=64)
             nc.vector.quantize_mx(
@@ -133,7 +146,7 @@ def tile_dummytemodel_pa_t_kernel(tc, hf, g1_w, g1_b, g2_w, g2_b, out):
             w_words, w_scales = codes[("w1", g, c)]
             y_planar = y_pool.tile([P, PACK, CHUNK], BF16, tag="y_planar")
             for j in range(PACK):
-                acc1 = psum_1.tile([P, CHUNK], F32, tag="acc1")
+                acc1 = psum_scalar.tile([P, BANK], F32, tag="bank")
                 nc.tensor.matmul_mx(
                     out=acc1[:],
                     lhsT=w_words[:, j * P : (j + 1) * P].bitcast(FP8X4),
@@ -144,12 +157,21 @@ def tile_dummytemodel_pa_t_kernel(tc, hf, g1_w, g1_b, g2_w, g2_b, out):
                     stop=True,
                 )
                 column = INNER_TILES * g + PACK * c + j
-                nc.scalar.activation(
-                    out=y_planar[:, j, :],
-                    in_=acc1[:],
-                    func=mybir.ActivationFunctionType.Identity,
-                    bias=b1_col[:, column : column + 1],
-                )
+                if s < ROUNDS_WITH_HELP and j % 2 == 1:
+                    nc.vector.tensor_scalar(
+                        out=y_planar[:, j, :],
+                        in0=acc1[:],
+                        scalar1=b1_col[:, column : column + 1],
+                        scalar2=None,
+                        op0=mybir.AluOpType.add,
+                    )
+                else:
+                    nc.scalar.activation(
+                        out=y_planar[:, j, :],
+                        in_=acc1[:],
+                        func=mybir.ActivationFunctionType.Identity,
+                        bias=b1_col[:, column : column + 1],
+                    )
             planar[(s, c)] = y_planar
 
         def regroup_y(s, c):
@@ -160,30 +182,29 @@ def tile_dummytemodel_pa_t_kernel(tc, hf, g1_w, g1_b, g2_w, g2_b, out):
             )
             grouped[("y", s, c)] = y_bf16
 
-        def layer2(s, blocks):
+        def layer2(s, b):
             g, n = divmod(s, CHUNKS_PER_GROUP)
-            for b in blocks:
-                acc2 = psum_2.tile([P, HIDDEN], F32, tag="acc2")
-                for c in range(PASSES_2):
-                    y_words, y_scales = codes[("y", s, c)]
-                    w_words, w_scales = codes[("w2", g, c)]
-                    nc.tensor.matmul_mx(
-                        out=acc2[:],
-                        lhsT=y_words[:, b * P : (b + 1) * P].bitcast(FP8X4),
-                        lhsT_scale=y_scales[:, b * P : (b + 1) * P],
-                        rhs=w_words[:].bitcast(FP8X4),
-                        rhs_scale=w_scales[:],
-                        start=(c == 0),
-                        stop=(c == PASSES_2 - 1),
-                    )
-                result = out_pool.tile([P, HIDDEN], F32, tag="result")
-                nc.vector.tensor_tensor(
-                    out=result[:],
-                    in0=acc2[:],
-                    in1=b2_all[:, g * HIDDEN : (g + 1) * HIDDEN],
-                    op=mybir.AluOpType.add,
+            acc2 = psum_vector.tile([P, HIDDEN], F32, tag="acc2")
+            for c in range(PASSES_2):
+                y_words, y_scales = codes[("y", s, c)]
+                w_words, w_scales = codes[("w2", g, c)]
+                nc.tensor.matmul_mx(
+                    out=acc2[:],
+                    lhsT=y_words[:, b * P : (b + 1) * P].bitcast(FP8X4),
+                    lhsT_scale=y_scales[:, b * P : (b + 1) * P],
+                    rhs=w_words[:].bitcast(FP8X4),
+                    rhs_scale=w_scales[:],
+                    start=(c == 0),
+                    stop=(c == PASSES_2 - 1),
                 )
-                nc.sync.dma_start(out=out_view[g, :, n * BLOCKS + b, :], in_=result[:])
+            result = out_pool.tile([P, HIDDEN], F32, tag="result")
+            nc.vector.tensor_tensor(
+                out=result[:],
+                in0=acc2[:],
+                in1=b2_all[:, g * HIDDEN : (g + 1) * HIDDEN],
+                op=mybir.AluOpType.add,
+            )
+            nc.sync.dma_start(out=out_view[g, :, n * BLOCKS + b, :], in_=result[:])
 
         units = []
         for g in range(GROUPS):
@@ -194,37 +215,42 @@ def tile_dummytemodel_pa_t_kernel(tc, hf, g1_w, g1_b, g2_w, g2_b, out):
 
         for i in range(LEAD):
             transpose_unit(units[i])
-            if i > 0:
-                quantise(units[i - 1], units[i - 1][0])
-        quantise(units[LEAD - 1], units[LEAD - 1][0])
+            if i == 0:
+                transpose_bias()
+            else:
+                quantise(units[i - 1])
+        quantise(units[LEAD - 1])
 
         for s in range(CHUNKS + 1):
             first = LEAD + UNITS_PER_ROUND * s
             unit_a, unit_b, unit_c = units[first : first + 1], units[first + 1 : first + 2], units[first + 2 : first + 3]
-            if s < CHUNKS:
+            here, behind = s < CHUNKS, s > 0
+            if here:
                 layer1(s, 0)
             for key in unit_a:
                 transpose_unit(key)
-            if s < CHUNKS:
+            if behind:
+                layer2(s - 1, 0)
+            if here:
                 regroup_y(s, 0)
-                layer1(s, 1)
             for key in unit_a:
-                quantise(key, key[0])
-            for key in unit_b:
+                quantise(key)
+            if here:
+                layer1(s, 1)
+            if behind:
+                layer2(s - 1, 1)
+            if here:
+                quantise(("y", s, 0))
+            for key in unit_b + unit_c:
                 transpose_unit(key)
-            if s < CHUNKS:
-                quantise(("y", s, 0), "y")
-            if s > 0:
-                layer2(s - 1, range(0, BLOCKS // 2))
-            if s < CHUNKS:
+            if here:
                 regroup_y(s, 1)
             for key in unit_b:
-                quantise(key, key[0])
-            if s > 0:
-                layer2(s - 1, range(BLOCKS // 2, BLOCKS))
+                quantise(key)
+            if here:
+                quantise(("y", s, 1))
             for key in unit_c:
-                transpose_unit(key)
-            if s < CHUNKS:
-                quantise(("y", s, 1), "y")
-            for key in unit_c:
-                quantise(key, key[0])
+                quantise(key)
+            if behind:
+                layer2(s - 1, 2)
+                layer2(s - 1, 3)

@@ -39,7 +39,7 @@ def tile_dummytemodel_pa_t_kernel(tc, hf, g1_w, g1_b, g2_w, g2_b, out):
         grouped_pool = ctx.enter_context(tc.tile_pool(name="grouped", bufs=3))
         codes_pool = ctx.enter_context(tc.tile_pool(name="codes", bufs=4))
         y_pool = ctx.enter_context(tc.tile_pool(name="y", bufs=3))
-        out_pool = ctx.enter_context(tc.tile_pool(name="outs", bufs=6))
+        out_pool = ctx.enter_context(tc.tile_pool(name="outs", bufs=12))
         psum_scalar = ctx.enter_context(tc.psum_pool(name="psum_scalar", bufs=5))
         psum_vector = ctx.enter_context(tc.psum_pool(name="psum_vector", bufs=3))
         ctx.enter_context(tc.manual_schedule())
@@ -59,7 +59,9 @@ def tile_dummytemodel_pa_t_kernel(tc, hf, g1_w, g1_b, g2_w, g2_b, out):
             out=b1_rows[:].bitcast(BF16)[0 : GROUPS * 4, :],
             in_=g1_b.rearrange("g (cu w) -> (g cu) w", w=2 * P),
         )
-        b2_all = const.tile([P, GROUPS * HIDDEN], BF16)
+        b2_rows = const.tile([P, GROUPS * HIDDEN], BF16)
+        nc.vector.memset(b2_rows[:], 0.0)
+        nc.scalar.dma_start(out=b2_rows[0:1, :], in_=g2_b.rearrange("(o g) h -> o (g h)", o=1))
 
         def load_x(s):
             g, n = divmod(s, CHUNKS_PER_GROUP)
@@ -82,8 +84,6 @@ def tile_dummytemodel_pa_t_kernel(tc, hf, g1_w, g1_b, g2_w, g2_b, out):
                 load_w1(g, c)
             load_x(CHUNKS_PER_GROUP * g + 1)
             nc.sync.dma_start(out=w2_sb[g][:], in_=w2_view[g])
-            if g == 0:
-                nc.sync.dma_start(out=b2_all[:], in_=g2_b.rearrange("g h -> (g h)").partition_broadcast(P))
 
         ident = const.tile([P, P], F32)
         make_identity(nc, ident[:])
@@ -96,6 +96,16 @@ def tile_dummytemodel_pa_t_kernel(tc, hf, g1_w, g1_b, g2_w, g2_b, out):
             nc.tensor.transpose(b1_bank[:, 0:P], b1_rows[:], ident[:])
             nc.vector.tensor_copy(out=b1_words[:], in_=b1_bank[:, 0 : GROUPS * 4])
             nc.vector.tensor_copy(out=b1_col[:], in_=b1_words[:].bitcast(BF16))
+
+        ones = const.tile([P, P], BF16)
+        nc.vector.memset(ones[:], 1.0)
+        b2_all = const.tile([P, GROUPS * HIDDEN], BF16)
+
+        def spread_bias2(g):
+            columns = slice(g * HIDDEN, (g + 1) * HIDDEN)
+            spread = psum_vector.tile([P, HIDDEN], BF16, tag="acc2")
+            nc.tensor.matmul(out=spread[:], lhsT=ones[:], rhs=b2_rows[:, columns], start=True, stop=True)
+            nc.vector.tensor_copy(out=b2_all[:, columns], in_=spread[:])
 
         def unit_blocks(key):
             kind = key[0]
@@ -225,6 +235,8 @@ def tile_dummytemodel_pa_t_kernel(tc, hf, g1_w, g1_b, g2_w, g2_b, out):
             first = LEAD + UNITS_PER_ROUND * s
             unit_a, unit_b, unit_c = units[first : first + 1], units[first + 1 : first + 2], units[first + 2 : first + 3]
             here, behind = s < CHUNKS, s > 0
+            if here and s % CHUNKS_PER_GROUP == 0:
+                spread_bias2(s // CHUNKS_PER_GROUP)
             if here:
                 layer1(s, 0)
             for key in unit_a:

@@ -27,6 +27,7 @@ INNER_TILES = INNER // P
 LEAD = 4
 UNITS_PER_ROUND = 3
 ROUNDS_WITH_HELP = 1
+BIAS2_BEHIND = (1, 0)
 
 FLOPS = 2 * TOKENS * HIDDEN * INNER * 2
 
@@ -59,9 +60,7 @@ def tile_dummytemodel_pa_t_kernel(tc, hf, g1_w, g1_b, g2_w, g2_b, out):
             out=b1_rows[:].bitcast(BF16)[0 : GROUPS * 4, :],
             in_=g1_b.rearrange("g (cu w) -> (g cu) w", w=2 * P),
         )
-        b2_rows = const.tile([P, GROUPS * HIDDEN], BF16)
-        nc.vector.memset(b2_rows[:], 0.0)
-        nc.scalar.dma_start(out=b2_rows[0:1, :], in_=g2_b.rearrange("(o g) h -> o (g h)", o=1))
+        b2_all = const.tile([P, GROUPS * HIDDEN], BF16)
 
         def load_x(s):
             g, n = divmod(s, CHUNKS_PER_GROUP)
@@ -82,6 +81,8 @@ def tile_dummytemodel_pa_t_kernel(tc, hf, g1_w, g1_b, g2_w, g2_b, out):
             load_x(CHUNKS_PER_GROUP * g)
             for c in range(PASSES_2):
                 load_w1(g, c)
+                if (g, c) == BIAS2_BEHIND:
+                    nc.sync.dma_start(out=b2_all[:], in_=g2_b.rearrange("g h -> (g h)").partition_broadcast(P))
             load_x(CHUNKS_PER_GROUP * g + 1)
             nc.sync.dma_start(out=w2_sb[g][:], in_=w2_view[g])
 
@@ -96,16 +97,6 @@ def tile_dummytemodel_pa_t_kernel(tc, hf, g1_w, g1_b, g2_w, g2_b, out):
             nc.tensor.transpose(b1_bank[:, 0:P], b1_rows[:], ident[:])
             nc.vector.tensor_copy(out=b1_words[:], in_=b1_bank[:, 0 : GROUPS * 4])
             nc.vector.tensor_copy(out=b1_col[:], in_=b1_words[:].bitcast(BF16))
-
-        ones = const.tile([P, P], BF16)
-        nc.vector.memset(ones[:], 1.0)
-        b2_all = const.tile([P, GROUPS * HIDDEN], BF16)
-
-        def spread_bias2(g):
-            columns = slice(g * HIDDEN, (g + 1) * HIDDEN)
-            spread = psum_vector.tile([P, HIDDEN], BF16, tag="acc2")
-            nc.tensor.matmul(out=spread[:], lhsT=ones[:], rhs=b2_rows[:, columns], start=True, stop=True)
-            nc.vector.tensor_copy(out=b2_all[:, columns], in_=spread[:])
 
         def unit_blocks(key):
             kind = key[0]
@@ -235,8 +226,6 @@ def tile_dummytemodel_pa_t_kernel(tc, hf, g1_w, g1_b, g2_w, g2_b, out):
             first = LEAD + UNITS_PER_ROUND * s
             unit_a, unit_b, unit_c = units[first : first + 1], units[first + 1 : first + 2], units[first + 2 : first + 3]
             here, behind = s < CHUNKS, s > 0
-            if here and s % CHUNKS_PER_GROUP == 0:
-                spread_bias2(s // CHUNKS_PER_GROUP)
             if here:
                 layer1(s, 0)
             for key in unit_a:

from contextlib import ExitStack

import concourse.mybir as mybir
from concourse.masks import make_identity

F32 = mybir.dt.float32
BF16 = mybir.dt.bfloat16
U32 = mybir.dt.uint32
U8 = mybir.dt.uint8
FP8X4 = mybir.dt.float8_e4m3fn_x4

P = 128
PACK = 4
K_PASS = P * PACK
WORDS = K_PASS // 2
BANK = 512

GROUPS, TOKENS, HIDDEN, INNER = 4, 4096, 512, 1024
GROUP_TOKENS = TOKENS // GROUPS
CHUNK = 512
CHUNKS = TOKENS // CHUNK
CHUNKS_PER_GROUP = GROUP_TOKENS // CHUNK
BLOCKS = CHUNK // P
PASSES_2 = INNER // K_PASS
INNER_TILES = INNER // P

LEAD = 4
UNITS_PER_ROUND = 3
ROUNDS_WITH_HELP = 1
BIAS2_BEHIND = (1, 0)

FLOPS = 2 * TOKENS * HIDDEN * INNER * 2


def tile_dummytemodel_pa_t_kernel(tc, hf, g1_w, g1_b, g2_w, g2_b, out):
    nc = tc.nc
    with ExitStack() as ctx:
        const = ctx.enter_context(tc.tile_pool(name="const", bufs=1))
        inputs = ctx.enter_context(tc.tile_pool(name="inputs", bufs=1))
        grouped_pool = ctx.enter_context(tc.tile_pool(name="grouped", bufs=3))
        codes_pool = ctx.enter_context(tc.tile_pool(name="codes", bufs=4))
        y_pool = ctx.enter_context(tc.tile_pool(name="y", bufs=3))
        out_pool = ctx.enter_context(tc.tile_pool(name="outs", bufs=12))
        psum_scalar = ctx.enter_context(tc.psum_pool(name="psum_scalar", bufs=5))
        psum_vector = ctx.enter_context(tc.psum_pool(name="psum_vector", bufs=3))
        ctx.enter_context(tc.manual_schedule())

        hf_view = hf.rearrange("(g r a) k -> g r a k", g=GROUPS, r=P)
        out_view = out.rearrange("(g r a) h -> g r a h", g=GROUPS, r=P)
        w1_view = g1_w.rearrange("g (cu r e) k -> g r cu (e k)", r=P, e=2)
        w2_view = g2_w.rearrange("g (b r) i -> g r b i", r=P)

        x_sb = [inputs.tile([P, BLOCKS, HIDDEN], BF16, name="x_sb%d" % s) for s in range(CHUNKS)]
        w1_sb = [inputs.tile([P, INNER_TILES, HIDDEN], BF16, name="w1_sb%d" % g) for g in range(GROUPS)]
        w2_sb = [inputs.tile([P, HIDDEN // P, INNER], BF16, name="w2_sb%d" % g) for g in range(GROUPS)]

        b1_rows = const.tile([P, P], F32)
        nc.vector.memset(b1_rows[:], 0.0)
        nc.scalar.dma_start(
            out=b1_rows[:].bitcast(BF16)[0 : GROUPS * 4, :],
            in_=g1_b.rearrange("g (cu w) -> (g cu) w", w=2 * P),
        )
        b2_all = const.tile([P, GROUPS * HIDDEN], BF16)

        def load_x(s):
            g, n = divmod(s, CHUNKS_PER_GROUP)
            for half in range(2):
                nc.sync.dma_start(
                    out=x_sb[s][:, 2 * half : 2 * half + 2, :],
                    in_=hf_view[g, :, n * BLOCKS + 2 * half : n * BLOCKS + 2 * half + 2, :],
                )

        def load_w1(g, c):
            for u in range(2):
                nc.sync.dma_start(
                    out=w1_sb[g][:, PACK * c + 2 * u : PACK * c + 2 * u + 2, :].rearrange("p e k -> p (e k)"),
                    in_=w1_view[g, :, 2 * c + u, :],
                )

        for g in range(GROUPS):
            load_x(CHUNKS_PER_GROUP * g)
            for c in range(PASSES_2):
                load_w1(g, c)
                if (g, c) == BIAS2_BEHIND:
                    nc.sync.dma_start(out=b2_all[:], in_=g2_b.rearrange("g h -> (g h)").partition_broadcast(P))
            load_x(CHUNKS_PER_GROUP * g + 1)
            nc.sync.dma_start(out=w2_sb[g][:], in_=w2_view[g])

        ident = const.tile([P, P], F32)
        make_identity(nc, ident[:])

        b1_words = const.tile([P, GROUPS * 4], F32)
        b1_col = const.tile([P, GROUPS * INNER_TILES], F32)

        def transpose_bias():
            b1_bank = psum_scalar.tile([P, BANK], F32, tag="bank")
            nc.tensor.transpose(b1_bank[:, 0:P], b1_rows[:], ident[:])
            nc.vector.tensor_copy(out=b1_words[:], in_=b1_bank[:, 0 : GROUPS * 4])
            nc.vector.tensor_copy(out=b1_col[:], in_=b1_words[:].bitcast(BF16))

        def unit_blocks(key):
            kind = key[0]
            if kind == "x":
                words = x_sb[key[1]][:].bitcast(F32)
                return [words[:, a, :] for a in range(BLOCKS)]
            if kind == "w1":
                words = w1_sb[key[1]][:].bitcast(F32)
                return [words[:, PACK * key[2] + j, :] for j in range(PACK)]
            words = w2_sb[key[1]][:].bitcast(F32)
            return [words[:, b, WORDS * key[2] : WORDS * (key[2] + 1)] for b in range(HIDDEN // P)]

        grouped = {}
        codes = {}

        def transpose_unit(key):
            blocks = unit_blocks(key)
            unit_bf16 = grouped_pool.tile([P, CHUNK, PACK], BF16, tag="unit_bf16", align_bytes=64)
            unit_words = unit_bf16[:].bitcast(F32)
            for half in range(2):
                bank = psum_scalar.tile([P, BANK], F32, tag="bank")
                planes = bank[:].rearrange("p (b u r) -> p b u r", b=2, u=2)
                for b in range(2):
                    for u in range(2):
                        nc.tensor.transpose(planes[:, b, u, :], blocks[2 * half + b][:, u * P : (u + 1) * P], ident[:])
                nc.scalar.copy(
                    out=unit_words[:, 2 * P * half : 2 * P * (half + 1), :].rearrange("p (b r) u -> p b r u", b=2),
                    in_=planes.rearrange("p b u r -> p b r u"),
                )
            grouped[key] = unit_bf16

        def quantise(key):
            tag = key[0]
            words = codes_pool.tile([P, CHUNK], U32, tag=tag + "_words", align_bytes=64)
            scales = codes_pool.tile([P, CHUNK], U8, tag=tag + "_scales", align_bytes=64)
            nc.vector.quantize_mx(
                out=words[:].bitcast(FP8X4),
                scales=scales[:],
                in_=grouped[key][:].rearrange("p c j -> p (c j)"),
            )
            codes[key] = (words, scales)

        planar = {}

        def layer1(s, c):
            g = s // CHUNKS_PER_GROUP
            x_words, x_scales = codes[("x", s)]
            w_words, w_scales = codes[("w1", g, c)]
            y_planar = y_pool.tile([P, PACK, CHUNK], BF16, tag="y_planar")
            for j in range(PACK):
                acc1 = psum_scalar.tile([P, BANK], F32, tag="bank")
                nc.tensor.matmul_mx(
                    out=acc1[:],
                    lhsT=w_words[:, j * P : (j + 1) * P].bitcast(FP8X4),
                    lhsT_scale=w_scales[:, j * P : (j + 1) * P],
                    rhs=x_words[:].bitcast(FP8X4),
                    rhs_scale=x_scales[:],
                    start=True,
                    stop=True,
                )
                column = INNER_TILES * g + PACK * c + j
                if s < ROUNDS_WITH_HELP and j % 2 == 1:
                    nc.vector.tensor_scalar(
                        out=y_planar[:, j, :],
                        in0=acc1[:],
                        scalar1=b1_col[:, column : column + 1],
                        scalar2=None,
                        op0=mybir.AluOpType.add,
                    )
                else:
                    nc.scalar.activation(
                        out=y_planar[:, j, :],
                        in_=acc1[:],
                        func=mybir.ActivationFunctionType.Identity,
                        bias=b1_col[:, column : column + 1],
                    )
            planar[(s, c)] = y_planar

        def regroup_y(s, c):
            y_bf16 = y_pool.tile([P, CHUNK, PACK], BF16, tag="y_bf16", align_bytes=64)
            nc.vector.tensor_copy(
                out=y_bf16[:].rearrange("p (t i) j -> p t j i", i=4),
                in_=planar[(s, c)][:].rearrange("p j (t i) -> p t j i", i=4),
            )
            grouped[("y", s, c)] = y_bf16

        def layer2(s, b):
            g, n = divmod(s, CHUNKS_PER_GROUP)
            acc2 = psum_vector.tile([P, HIDDEN], F32, tag="acc2")
            for c in range(PASSES_2):
                y_words, y_scales = codes[("y", s, c)]
                w_words, w_scales = codes[("w2", g, c)]
                nc.tensor.matmul_mx(
                    out=acc2[:],
                    lhsT=y_words[:, b * P : (b + 1) * P].bitcast(FP8X4),
                    lhsT_scale=y_scales[:, b * P : (b + 1) * P],
                    rhs=w_words[:].bitcast(FP8X4),
                    rhs_scale=w_scales[:],
                    start=(c == 0),
                    stop=(c == PASSES_2 - 1),
                )
            result = out_pool.tile([P, HIDDEN], F32, tag="result")
            nc.vector.tensor_tensor(
                out=result[:],
                in0=acc2[:],
                in1=b2_all[:, g * HIDDEN : (g + 1) * HIDDEN],
                op=mybir.AluOpType.add,
            )
            nc.sync.dma_start(out=out_view[g, :, n * BLOCKS + b, :], in_=result[:])

        units = []
        for g in range(GROUPS):
            units.append(("x", CHUNKS_PER_GROUP * g))
            units.extend([("w1", g, c) for c in range(PASSES_2)])
            units.append(("x", CHUNKS_PER_GROUP * g + 1))
            units.extend([("w2", g, c) for c in range(PASSES_2)])

        for i in range(LEAD):
            transpose_unit(units[i])
            if i == 0:
                transpose_bias()
            else:
                quantise(units[i - 1])
        quantise(units[LEAD - 1])

        for s in range(CHUNKS + 1):
            first = LEAD + UNITS_PER_ROUND * s
            unit_a, unit_b, unit_c = units[first : first + 1], units[first + 1 : first + 2], units[first + 2 : first + 3]
            here, behind = s < CHUNKS, s > 0
            if here:
                layer1(s, 0)
            for key in unit_a:
                transpose_unit(key)
            if behind:
                layer2(s - 1, 0)
            if here:
                regroup_y(s, 0)
            for key in unit_a:
                quantise(key)
            if here:
                layer1(s, 1)
            if behind:
                layer2(s - 1, 1)
            if here:
                quantise(("y", s, 0))
            for key in unit_b + unit_c:
                transpose_unit(key)
            if here:
                regroup_y(s, 1)
            for key in unit_b:
                quantise(key)
            if here:
                quantise(("y", s, 1))
            for key in unit_c:
                quantise(key)
            if behind:
                layer2(s - 1, 2)
                layer2(s - 1, 3)
